import numpy as np
import ml_dtypes


def mxq(x, axis, fmt="e4m3"):
    dtype, down = {"e4m3": (ml_dtypes.float8_e4m3fn, 7), "e5m2": (ml_dtypes.float8_e5m2, 14)}[fmt]
    v = np.moveaxis(np.asarray(x, np.float32).astype(ml_dtypes.bfloat16).astype(np.float64), axis, -1)
    blocks = v.reshape(v.shape[:-1] + (-1, 32))
    amax = np.abs(blocks).max(-1, keepdims=True)
    byte = np.maximum(np.where(amax > 0, np.frexp(amax)[1] - 1 + 127, 0) - down, 1)
    scale = np.exp2(byte - 127.0)
    codes = (blocks / scale).astype(np.float32).astype(dtype).astype(np.float64)
    return np.moveaxis((codes * scale).reshape(v.shape), -1, axis)


BF16 = ml_dtypes.bfloat16


def bf(x):
    return np.asarray(x, np.float32).astype(BF16)


def f64(x):
    return np.asarray(x).astype(np.float64)


B, C_IN, C_OUT, H, W = 1, 1024, 128, 112, 112
SC = 1.0 / np.sqrt(np.sqrt(C_IN))


def sign_ste(v, alpha):
    est = np.tanh(alpha * v)
    return (np.sign(v) - est) + est


def setup_inputs():
    return {"x": bf(np.random.standard_normal((B, C_IN, H, W)) * SC),
            "weight": bf(np.random.standard_normal((C_OUT, C_IN, 1, 1)) * SC),
            "alpha_x": bf(1.0 + 0.1 * np.random.standard_normal(1)),
            "alpha_w": bf(1.0 + 0.1 * np.random.standard_normal(1))}


def reference(x, weight, alpha_x, alpha_w):
    x, weight, alpha_x, alpha_w = f64(x), f64(weight), f64(alpha_x), f64(alpha_w)
    b, c, h, w = x.shape
    out_ch = weight.shape[0]
    x_unf = x.reshape(b, c, h * w).transpose(0, 2, 1)
    w_unf = weight.reshape(out_ch, c).T
    signxw = mxq(sign_ste(x_unf, alpha_x), 2, "e4m3") @ mxq(w_unf, 0, "e4m3")
    signwx = mxq(x_unf, 2, "e4m3") @ mxq(sign_ste(w_unf, alpha_w), 0, "e4m3")
    return (signxw + signwx).transpose(0, 2, 1).reshape(b, out_ch, h, w)

@@ -1,0 +1,160 @@
+from contextlib import ExitStack
+
+import concourse.mybir as mybir
+from concourse.masks import make_identity
+
+BF16 = mybir.dt.bfloat16
+F32 = mybir.dt.float32
+U32 = mybir.dt.uint32
+U8 = mybir.dt.uint8
+FP8X4 = mybir.dt.float8_e4m3fn_x4
+SIGN = mybir.ActivationFunctionType.Sign
+
+P = 128
+PACK = 4
+K_PASS = P * PACK
+C_IN = 1024
+C_OUT = 128
+PASSES = C_IN // K_PASS
+COLS = 112 * 112
+W_MAX = 1024
+N_MAX = 512
+CHUNKS = [256, 512] + [W_MAX] * 11 + [256, 256]
+assert sum(CHUNKS) == COLS
+VECTOR_BANK_EVERY = 3
+LOAD_AHEAD = 2
+
+FLOPS = 2 * 2 * C_IN * C_OUT * COLS
+
+
+def tile_pointwise_t_kernel(tc, x, weight, alpha_x, alpha_w, out):
+    nc = tc.nc
+    x_rows = x.rearrange("b c h w -> (b c) (h w)")
+    w_rows = weight.rearrange("o c a b -> o (c a b)")
+    out_rows = out.rearrange("b o h w -> (b o) (h w)")
+
+    starts = [sum(CHUNKS[:i]) for i in range(len(CHUNKS))]
+    units = [(i, g) for i in range(len(CHUNKS)) for g in range(PASSES)]
+
+    with ExitStack() as stack:
+        const = stack.enter_context(tc.tile_pool(name="const", bufs=1))
+        raw_pool = stack.enter_context(tc.tile_pool(name="raw", bufs=2 * (LOAD_AHEAD + 1)))
+        group_pool = stack.enter_context(tc.tile_pool(name="group", bufs=5))
+        code_pool = stack.enter_context(tc.tile_pool(name="code", bufs=4))
+        res_pool = stack.enter_context(tc.tile_pool(name="res", bufs=3))
+        psum_w = stack.enter_context(tc.psum_pool(name="psum_w", bufs=1))
+        psum = stack.enter_context(tc.psum_pool(name="psum", bufs=4))
+
+        raw = {}
+        x_grouped = {}
+        s_grouped = {}
+        x_codes = {}
+        s_codes = {}
+
+        def load(i):
+            for g in range(PASSES):
+                t = raw_pool.tile([P, PACK, W_MAX], BF16, name="raw_t", tag="raw")
+                raw[(i, g)] = t
+                nc.sync.dma_start(
+                    out=t[:, :, : CHUNKS[i]],
+                    in_=x_rows[K_PASS * g : K_PASS * (g + 1), starts[i] : starts[i] + CHUNKS[i]].rearrange(
+                        "(p j) w -> p j w", j=PACK
+                    ),
+                )
+
+        def regroup_and_sign(i, g):
+            w = CHUNKS[i]
+            xg = group_pool.tile([P, PACK * W_MAX], BF16, name="xg_t", tag="xg", align_bytes=64)
+            sg = group_pool.tile([P, PACK * W_MAX], BF16, name="sg_t", tag="sg", align_bytes=64)
+            x_grouped[(i, g)] = xg
+            s_grouped[(i, g)] = sg
+            nc.vector.tensor_copy(
+                out=xg[:, : PACK * w].rearrange("p (c i j) -> p c j i", i=4, j=PACK),
+                in_=raw[(i, g)][:, :, :w].rearrange("p j (c i) -> p c j i", i=4),
+            )
+            nc.scalar.activation(out=sg[:, : PACK * w], in_=xg[:, : PACK * w], func=SIGN)
+
+        def quantise(i, g, grouped, store, tag):
+            w = CHUNKS[i]
+            codes = code_pool.tile([P, W_MAX], U32, name=tag + "_codes", tag=tag + "c", align_bytes=64)
+            scales = code_pool.tile([P, W_MAX], U8, name=tag + "_scales", tag=tag + "s", align_bytes=64)
+            store[(i, g)] = (codes, scales)
+            nc.vector.quantize_mx(
+                out=codes[:, :w].bitcast(FP8X4), scales=scales[:, :w], in_=grouped[(i, g)][:, : PACK * w]
+            )
+
+        banks = [0]
+
+        def multiply_and_store(i):
+            w = CHUNKS[i]
+            n = min(w, N_MAX)
+            res = res_pool.tile([P, W_MAX], F32, name="res_t", tag="res")
+            for h in range(w // n):
+                cols = slice(h * n, (h + 1) * n)
+                acc = psum.tile([P, N_MAX], F32, name="acc_t", tag="acc")
+                steps = []
+                for g in range(PASSES):
+                    steps.append((w_q, g, s_codes[(i, g)]))
+                    steps.append((sw_q, g, x_codes[(i, g)]))
+                for k, (stat, g, (codes, scales)) in enumerate(steps):
+                    o_cols = slice(g * C_OUT, (g + 1) * C_OUT)
+                    nc.tensor.matmul_mx(
+                        out=acc[:, :n],
+                        lhsT=stat[0][:, o_cols].bitcast(FP8X4),
+                        lhsT_scale=stat[1][:, o_cols],
+                        rhs=codes[:, cols].bitcast(FP8X4),
+                        rhs_scale=scales[:, cols],
+                        start=(k == 0),
+                        stop=(k == len(steps) - 1),
+                    )
+                if banks[0] % VECTOR_BANK_EVERY == VECTOR_BANK_EVERY - 1:
+                    nc.vector.tensor_copy(out=res[:, cols], in_=acc[:, :n])
+                else:
+                    nc.scalar.copy(out=res[:, cols], in_=acc[:, :n])
+                banks[0] += 1
+            nc.sync.dma_start(out=out_rows[:, starts[i] : starts[i] + w], in_=res[:, :w])
+
+        for i in range(LOAD_AHEAD):
+            load(i)
+
+        ident = const.tile([P, P], F32)
+        make_identity(nc, ident[:])
+        w_sb = const.tile([P, C_IN], BF16)
+        nc.scalar.dma_start(out=w_sb[:], in_=w_rows)
+        w_words = w_sb[:].bitcast(F32).rearrange("o (g p u) -> o g u p", g=PASSES, u=2)
+        w_t = psum_w.tile([P, PASSES * 2, C_OUT], F32)
+        for g in range(PASSES):
+            for u in range(2):
+                nc.tensor.transpose(w_t[:, 2 * g + u, :], w_words[:, g, u, :], ident[:])
+        w_grouped = const.tile([P, PASSES * C_OUT * PACK], BF16, align_bytes=64)
+        sw_grouped = const.tile([P, PASSES * C_OUT * PACK], BF16, align_bytes=64)
+        nc.vector.tensor_copy(
+            out=w_grouped[:].bitcast(F32).rearrange("p (g o u) -> p g o u", g=PASSES, u=2),
+            in_=w_t[:].rearrange("p (g u) o -> p g o u", u=2),
+        )
+        nc.scalar.activation(out=sw_grouped[:], in_=w_grouped[:], func=SIGN)
+        w_q = (
+            const.tile([P, PASSES * C_OUT], U32, name="w_codes", align_bytes=64),
+            const.tile([P, PASSES * C_OUT], U8, name="w_scales", align_bytes=64),
+        )
+        sw_q = (
+            const.tile([P, PASSES * C_OUT], U32, name="sw_codes", align_bytes=64),
+            const.tile([P, PASSES * C_OUT], U8, name="sw_scales", align_bytes=64),
+        )
+        nc.vector.quantize_mx(out=w_q[0][:].bitcast(FP8X4), scales=w_q[1][:], in_=w_grouped[:])
+        nc.vector.quantize_mx(out=sw_q[0][:].bitcast(FP8X4), scales=sw_q[1][:], in_=sw_grouped[:])
+
+        for u in range(len(units) + 2):
+            if u < len(units):
+                i, g = units[u]
+                if g == 0 and i + LOAD_AHEAD < len(CHUNKS):
+                    load(i + LOAD_AHEAD)
+                regroup_and_sign(i, g)
+            if 1 <= u <= len(units):
+                i, g = units[u - 1]
+                quantise(i, g, x_grouped, x_codes, "x")
+            if u >= 2:
+                i, g = units[u - 2]
+                quantise(i, g, s_grouped, s_codes, "s")
+                if g == PASSES - 1:
+                    multiply_and_store(i)

@@ -9,6 +9,9 @@ U32 = mybir.dt.uint32
 U8 = mybir.dt.uint8
 FP8X4 = mybir.dt.float8_e4m3fn_x4
 SIGN = mybir.ActivationFunctionType.Sign
+MULT = mybir.AluOpType.mult
+MIN = mybir.AluOpType.min
+MAX = mybir.AluOpType.max
 
 P = 128
 PACK = 4
@@ -21,7 +24,11 @@ W_MAX = 1024
 N_MAX = 512
 CHUNKS = [256, 512] + [W_MAX] * 11 + [256, 256]
 assert sum(CHUNKS) == COLS
-VECTOR_BANK_EVERY = 3
+VECTOR_BANK_EVERY = 12
+BLOCK = 128
+PE_BLOCKS = {(3, 1): 8, (5, 1): 8, (7, 1): 8, (9, 1): 8, (11, 1): 6}
+UP = 2.0**64
+TINY = 2.0**-69
 LOAD_AHEAD = 2
 
 FLOPS = 2 * 2 * C_IN * C_OUT * COLS
@@ -43,7 +50,9 @@ def tile_pointwise_t_kernel(tc, x, weight, alpha_x, alpha_w, out):
         code_pool = stack.enter_context(tc.tile_pool(name="code", bufs=4))
         res_pool = stack.enter_context(tc.tile_pool(name="res", bufs=3))
         psum_w = stack.enter_context(tc.psum_pool(name="psum_w", bufs=1))
-        psum = stack.enter_context(tc.psum_pool(name="psum", bufs=4))
+        psum = stack.enter_context(tc.psum_pool(name="psum", bufs=3))
+        psum_x = stack.enter_context(tc.psum_pool(name="psum_x", bufs=4))
+        tmp_pool = stack.enter_context(tc.tile_pool(name="tmp", bufs=2))
 
         raw = {}
         x_grouped = {}
@@ -68,11 +77,37 @@ def tile_pointwise_t_kernel(tc, x, weight, alpha_x, alpha_w, out):
             sg = group_pool.tile([P, PACK * W_MAX], BF16, name="sg_t", tag="sg", align_bytes=64)
             x_grouped[(i, g)] = xg
             s_grouped[(i, g)] = sg
-            nc.vector.tensor_copy(
-                out=xg[:, : PACK * w].rearrange("p (c i j) -> p c j i", i=4, j=PACK),
-                in_=raw[(i, g)][:, :, :w].rearrange("p j (c i) -> p c j i", i=4),
+            blocks = PE_BLOCKS.get((i, g), 0)
+            for b in range(0, blocks, 2):
+                bank = psum_x.tile([P, 2 * BLOCK * PACK], BF16, name="bank_t", tag="bank")
+                for h in range(2):
+                    n0 = BLOCK * (b + h)
+                    nc.tensor.matmul(
+                        out=bank[:, BLOCK * PACK * h : BLOCK * PACK * (h + 1)].rearrange("p (n j) -> p n j", j=PACK),
+                        lhsT=ident_bf[:],
+                        rhs=raw[(i, g)][:, :, n0 : n0 + BLOCK].rearrange("p j n -> p n j"),
+                        start=True,
+                        stop=True,
+                    )
+                nc.scalar.copy(out=xg[:, BLOCK * PACK * b : BLOCK * PACK * (b + 2)], in_=bank[:])
+            done = BLOCK * blocks
+            if done < w:
+                nc.vector.tensor_copy(
+                    out=xg[:, PACK * done : PACK * w].rearrange("p (c i j) -> p c j i", i=4, j=PACK),
+                    in_=raw[(i, g)][:, :, done:w].rearrange("p j (c i) -> p c j i", i=4),
+                )
+            if blocks == 0:
+                nc.scalar.activation(out=sg[:, : PACK * w], in_=xg[:, : PACK * w], func=SIGN)
+
+        def sign_on_vector(i, g):
+            w = CHUNKS[i]
+            big = tmp_pool.tile([P, PACK * W_MAX], BF16, name="big_t", tag="big")
+            nc.vector.tensor_scalar(
+                out=big[:, : PACK * w], in0=x_grouped[(i, g)][:, : PACK * w], scalar1=UP, scalar2=TINY, op0=MULT, op1=MIN
             )
-            nc.scalar.activation(out=sg[:, : PACK * w], in_=xg[:, : PACK * w], func=SIGN)
+            nc.vector.tensor_scalar(
+                out=s_grouped[(i, g)][:, : PACK * w], in0=big[:, : PACK * w], scalar1=-TINY, scalar2=1.0 / TINY, op0=MAX, op1=MULT
+            )
 
         def quantise(i, g, grouped, store, tag):
             w = CHUNKS[i]
@@ -119,6 +154,8 @@ def tile_pointwise_t_kernel(tc, x, weight, alpha_x, alpha_w, out):
 
         ident = const.tile([P, P], F32)
         make_identity(nc, ident[:])
+        ident_bf = const.tile([P, P], BF16)
+        make_identity(nc, ident_bf[:])
         w_sb = const.tile([P, C_IN], BF16)
         nc.scalar.dma_start(out=w_sb[:], in_=w_rows)
         w_words = w_sb[:].bitcast(F32).rearrange("o (g p u) -> o g u p", g=PASSES, u=2)
@@ -153,6 +190,8 @@ def tile_pointwise_t_kernel(tc, x, weight, alpha_x, alpha_w, out):
             if 1 <= u <= len(units):
                 i, g = units[u - 1]
                 quantise(i, g, x_grouped, x_codes, "x")
+                if (i, g) in PE_BLOCKS:
+                    sign_on_vector(i, g)
             if u >= 2:
                 i, g = units[u - 2]
                 quantise(i, g, s_grouped, s_codes, "s")

@@ -24,12 +24,14 @@ W_MAX = 1024
 N_MAX = 512
 CHUNKS = [256, 512] + [W_MAX] * 11 + [256, 256]
 assert sum(CHUNKS) == COLS
-VECTOR_BANK_EVERY = 12
+VECTOR_BANK_EVERY = 6
 BLOCK = 128
 PE_BLOCKS = {(3, 1): 8, (5, 1): 8, (7, 1): 8, (9, 1): 8, (11, 1): 6}
+VECTOR_SIGNS = [(3, 1), (7, 1), (11, 1)]
+BANKS_AHEAD = 4
 UP = 2.0**64
 TINY = 2.0**-69
-LOAD_AHEAD = 2
+LOAD_AHEAD = 3
 
 FLOPS = 2 * 2 * C_IN * C_OUT * COLS
 
@@ -45,20 +47,23 @@ def tile_pointwise_t_kernel(tc, x, weight, alpha_x, alpha_w, out):
 
     with ExitStack() as stack:
         const = stack.enter_context(tc.tile_pool(name="const", bufs=1))
-        raw_pool = stack.enter_context(tc.tile_pool(name="raw", bufs=2 * (LOAD_AHEAD + 1)))
+        raw_pool = stack.enter_context(tc.tile_pool(name="raw", bufs=2 * LOAD_AHEAD + 1))
         group_pool = stack.enter_context(tc.tile_pool(name="group", bufs=5))
-        code_pool = stack.enter_context(tc.tile_pool(name="code", bufs=4))
+        sign_pool = stack.enter_context(tc.tile_pool(name="sign", bufs=4))
+        early_pool = stack.enter_context(tc.tile_pool(name="early", bufs=2))
+        code_pool = stack.enter_context(tc.tile_pool(name="code", bufs=5))
         res_pool = stack.enter_context(tc.tile_pool(name="res", bufs=3))
         psum_w = stack.enter_context(tc.psum_pool(name="psum_w", bufs=1))
         psum = stack.enter_context(tc.psum_pool(name="psum", bufs=3))
         psum_x = stack.enter_context(tc.psum_pool(name="psum_x", bufs=4))
-        tmp_pool = stack.enter_context(tc.tile_pool(name="tmp", bufs=2))
+        tmp_pool = stack.enter_context(tc.tile_pool(name="tmp", bufs=1))
 
         raw = {}
         x_grouped = {}
         s_grouped = {}
         x_codes = {}
         s_codes = {}
+        lifted = {}
 
         def load(i):
             for g in range(PASSES):
@@ -71,42 +76,54 @@ def tile_pointwise_t_kernel(tc, x, weight, alpha_x, alpha_w, out):
                     ),
                 )
 
+        def regroup_bank(i, g, b):
+            if b == 0:
+                x_grouped[(i, g)] = early_pool.tile([P, PACK * W_MAX], BF16, name="xe_t", tag="xe", align_bytes=64)
+            bank = psum_x.tile([P, 2 * BLOCK * PACK], BF16, name="bank_t", tag="bank")
+            for h in range(2):
+                n0 = BLOCK * (2 * b + h)
+                nc.tensor.matmul(
+                    out=bank[:, BLOCK * PACK * h : BLOCK * PACK * (h + 1)].rearrange("p (n j) -> p n j", j=PACK),
+                    lhsT=ident_bf[:],
+                    rhs=raw[(i, g)][:, :, n0 : n0 + BLOCK].rearrange("p j n -> p n j"),
+                    start=True,
+                    stop=True,
+                )
+            nc.scalar.copy(out=x_grouped[(i, g)][:, 2 * BLOCK * PACK * b : 2 * BLOCK * PACK * (b + 1)], in_=bank[:])
+
         def regroup_and_sign(i, g):
             w = CHUNKS[i]
-            xg = group_pool.tile([P, PACK * W_MAX], BF16, name="xg_t", tag="xg", align_bytes=64)
-            sg = group_pool.tile([P, PACK * W_MAX], BF16, name="sg_t", tag="sg", align_bytes=64)
-            x_grouped[(i, g)] = xg
+            if (i, g) not in PE_BLOCKS:
+                x_grouped[(i, g)] = group_pool.tile([P, PACK * W_MAX], BF16, name="xg_t", tag="xg", align_bytes=64)
+            xg = x_grouped[(i, g)]
+            sg = sign_pool.tile([P, PACK * W_MAX], BF16, name="sg_t", tag="sg", align_bytes=64)
             s_grouped[(i, g)] = sg
-            blocks = PE_BLOCKS.get((i, g), 0)
-            for b in range(0, blocks, 2):
-                bank = psum_x.tile([P, 2 * BLOCK * PACK], BF16, name="bank_t", tag="bank")
-                for h in range(2):
-                    n0 = BLOCK * (b + h)
-                    nc.tensor.matmul(
-                        out=bank[:, BLOCK * PACK * h : BLOCK * PACK * (h + 1)].rearrange("p (n j) -> p n j", j=PACK),
-                        lhsT=ident_bf[:],
-                        rhs=raw[(i, g)][:, :, n0 : n0 + BLOCK].rearrange("p j n -> p n j"),
-                        start=True,
-                        stop=True,
-                    )
-                nc.scalar.copy(out=xg[:, BLOCK * PACK * b : BLOCK * PACK * (b + 2)], in_=bank[:])
-            done = BLOCK * blocks
+            done = BLOCK * PE_BLOCKS.get((i, g), 0)
             if done < w:
                 nc.vector.tensor_copy(
                     out=xg[:, PACK * done : PACK * w].rearrange("p (c i j) -> p c j i", i=4, j=PACK),
                     in_=raw[(i, g)][:, :, done:w].rearrange("p j (c i) -> p c j i", i=4),
                 )
-            if blocks == 0:
+            if (i, g) not in VECTOR_SIGNS:
                 nc.scalar.activation(out=sg[:, : PACK * w], in_=xg[:, : PACK * w], func=SIGN)
 
-        def sign_on_vector(i, g):
+        def sign_on_vector_first(i, g):
             w = CHUNKS[i]
             big = tmp_pool.tile([P, PACK * W_MAX], BF16, name="big_t", tag="big")
+            lifted[(i, g)] = big
             nc.vector.tensor_scalar(
                 out=big[:, : PACK * w], in0=x_grouped[(i, g)][:, : PACK * w], scalar1=UP, scalar2=TINY, op0=MULT, op1=MIN
             )
+
+        def sign_on_vector_second(i, g):
+            w = CHUNKS[i]
             nc.vector.tensor_scalar(
-                out=s_grouped[(i, g)][:, : PACK * w], in0=big[:, : PACK * w], scalar1=-TINY, scalar2=1.0 / TINY, op0=MAX, op1=MULT
+                out=s_grouped[(i, g)][:, : PACK * w],
+                in0=lifted[(i, g)][:, : PACK * w],
+                scalar1=-TINY,
+                scalar2=1.0 / TINY,
+                op0=MAX,
+                op1=MULT,
             )
 
         def quantise(i, g, grouped, store, tag):
@@ -181,19 +198,33 @@ def tile_pointwise_t_kernel(tc, x, weight, alpha_x, alpha_w, out):
         nc.vector.quantize_mx(out=w_q[0][:].bitcast(FP8X4), scales=w_q[1][:], in_=w_grouped[:])
         nc.vector.quantize_mx(out=sw_q[0][:].bitcast(FP8X4), scales=sw_q[1][:], in_=sw_grouped[:])
 
-        for u in range(len(units) + 2):
+        def quantise_sign_and_multiply(i, g):
+            quantise(i, g, s_grouped, s_codes, "s")
+            if g == PASSES - 1:
+                multiply_and_store(i)
+
+        for u in range(len(units) + 3):
             if u < len(units):
                 i, g = units[u]
                 if g == 0 and i + LOAD_AHEAD < len(CHUNKS):
                     load(i + LOAD_AHEAD)
+            for ahead in range(BANKS_AHEAD, 0, -1):
+                if u + ahead < len(units) and units[u + ahead] in PE_BLOCKS:
+                    b = BANKS_AHEAD - ahead
+                    if 2 * b < PE_BLOCKS[units[u + ahead]]:
+                        regroup_bank(units[u + ahead][0], units[u + ahead][1], b)
+            if u < len(units):
                 regroup_and_sign(i, g)
             if 1 <= u <= len(units):
                 i, g = units[u - 1]
                 quantise(i, g, x_grouped, x_codes, "x")
-                if (i, g) in PE_BLOCKS:
-                    sign_on_vector(i, g)
-            if u >= 2:
+                if (i, g) in VECTOR_SIGNS:
+                    sign_on_vector_first(i, g)
+            if 2 <= u <= len(units) + 1:
                 i, g = units[u - 2]
-                quantise(i, g, s_grouped, s_codes, "s")
-                if g == PASSES - 1:
-                    multiply_and_store(i)
+                if (i, g) in VECTOR_SIGNS:
+                    sign_on_vector_second(i, g)
+                else:
+                    quantise_sign_and_multiply(i, g)
+            if u >= 3 and units[u - 3] in VECTOR_SIGNS:
+                quantise_sign_and_multiply(units[u - 3][0], units[u - 3][1])

@@ -24,14 +24,10 @@ W_MAX = 1024
 N_MAX = 512
 CHUNKS = [256, 512] + [W_MAX] * 11 + [256, 256]
 assert sum(CHUNKS) == COLS
-VECTOR_BANK_EVERY = 6
-BLOCK = 128
-PE_BLOCKS = {(3, 1): 8, (5, 1): 8, (7, 1): 8, (9, 1): 8, (11, 1): 6}
-VECTOR_SIGNS = [(3, 1), (7, 1), (11, 1)]
-BANKS_AHEAD = 4
+VECTOR_SIGNS = [(8, 1), (13, 1), (14, 0), (14, 1)]
 UP = 2.0**64
 TINY = 2.0**-69
-LOAD_AHEAD = 3
+LOAD_AHEAD = 2
 
 FLOPS = 2 * 2 * C_IN * C_OUT * COLS
 
@@ -47,16 +43,14 @@ def tile_pointwise_t_kernel(tc, x, weight, alpha_x, alpha_w, out):
 
     with ExitStack() as stack:
         const = stack.enter_context(tc.tile_pool(name="const", bufs=1))
-        raw_pool = stack.enter_context(tc.tile_pool(name="raw", bufs=2 * LOAD_AHEAD + 1))
+        raw_pool = stack.enter_context(tc.tile_pool(name="raw", bufs=2 * (LOAD_AHEAD + 1)))
         group_pool = stack.enter_context(tc.tile_pool(name="group", bufs=5))
         sign_pool = stack.enter_context(tc.tile_pool(name="sign", bufs=4))
-        early_pool = stack.enter_context(tc.tile_pool(name="early", bufs=2))
         code_pool = stack.enter_context(tc.tile_pool(name="code", bufs=5))
         res_pool = stack.enter_context(tc.tile_pool(name="res", bufs=3))
         psum_w = stack.enter_context(tc.psum_pool(name="psum_w", bufs=1))
-        psum = stack.enter_context(tc.psum_pool(name="psum", bufs=3))
-        psum_x = stack.enter_context(tc.psum_pool(name="psum_x", bufs=4))
-        tmp_pool = stack.enter_context(tc.tile_pool(name="tmp", bufs=1))
+        psum = stack.enter_context(tc.psum_pool(name="psum", bufs=4))
+        tmp_pool = stack.enter_context(tc.tile_pool(name="tmp", bufs=2))
 
         raw = {}
         x_grouped = {}
@@ -76,34 +70,16 @@ def tile_pointwise_t_kernel(tc, x, weight, alpha_x, alpha_w, out):
                     ),
                 )
 
-        def regroup_bank(i, g, b):
-            if b == 0:
-                x_grouped[(i, g)] = early_pool.tile([P, PACK * W_MAX], BF16, name="xe_t", tag="xe", align_bytes=64)
-            bank = psum_x.tile([P, 2 * BLOCK * PACK], BF16, name="bank_t", tag="bank")
-            for h in range(2):
-                n0 = BLOCK * (2 * b + h)
-                nc.tensor.matmul(
-                    out=bank[:, BLOCK * PACK * h : BLOCK * PACK * (h + 1)].rearrange("p (n j) -> p n j", j=PACK),
-                    lhsT=ident_bf[:],
-                    rhs=raw[(i, g)][:, :, n0 : n0 + BLOCK].rearrange("p j n -> p n j"),
-                    start=True,
-                    stop=True,
-                )
-            nc.scalar.copy(out=x_grouped[(i, g)][:, 2 * BLOCK * PACK * b : 2 * BLOCK * PACK * (b + 1)], in_=bank[:])
-
         def regroup_and_sign(i, g):
             w = CHUNKS[i]
-            if (i, g) not in PE_BLOCKS:
-                x_grouped[(i, g)] = group_pool.tile([P, PACK * W_MAX], BF16, name="xg_t", tag="xg", align_bytes=64)
-            xg = x_grouped[(i, g)]
+            xg = group_pool.tile([P, PACK * W_MAX], BF16, name="xg_t", tag="xg", align_bytes=64)
+            x_grouped[(i, g)] = xg
             sg = sign_pool.tile([P, PACK * W_MAX], BF16, name="sg_t", tag="sg", align_bytes=64)
             s_grouped[(i, g)] = sg
-            done = BLOCK * PE_BLOCKS.get((i, g), 0)
-            if done < w:
-                nc.vector.tensor_copy(
-                    out=xg[:, PACK * done : PACK * w].rearrange("p (c i j) -> p c j i", i=4, j=PACK),
-                    in_=raw[(i, g)][:, :, done:w].rearrange("p j (c i) -> p c j i", i=4),
-                )
+            nc.vector.tensor_copy(
+                out=xg[:, : PACK * w].rearrange("p (c i j) -> p c j i", i=4, j=PACK),
+                in_=raw[(i, g)][:, :, :w].rearrange("p j (c i) -> p c j i", i=4),
+            )
             if (i, g) not in VECTOR_SIGNS:
                 nc.scalar.activation(out=sg[:, : PACK * w], in_=xg[:, : PACK * w], func=SIGN)
 
@@ -135,8 +111,6 @@ def tile_pointwise_t_kernel(tc, x, weight, alpha_x, alpha_w, out):
                 out=codes[:, :w].bitcast(FP8X4), scales=scales[:, :w], in_=grouped[(i, g)][:, : PACK * w]
             )
 
-        banks = [0]
-
         def multiply_and_store(i):
             w = CHUNKS[i]
             n = min(w, N_MAX)
@@ -159,11 +133,7 @@ def tile_pointwise_t_kernel(tc, x, weight, alpha_x, alpha_w, out):
                         start=(k == 0),
                         stop=(k == len(steps) - 1),
                     )
-                if banks[0] % VECTOR_BANK_EVERY == VECTOR_BANK_EVERY - 1:
-                    nc.vector.tensor_copy(out=res[:, cols], in_=acc[:, :n])
-                else:
-                    nc.scalar.copy(out=res[:, cols], in_=acc[:, :n])
-                banks[0] += 1
+                nc.scalar.copy(out=res[:, cols], in_=acc[:, :n])
             nc.sync.dma_start(out=out_rows[:, starts[i] : starts[i] + w], in_=res[:, :w])
 
         for i in range(LOAD_AHEAD):
@@ -171,8 +141,6 @@ def tile_pointwise_t_kernel(tc, x, weight, alpha_x, alpha_w, out):
 
         ident = const.tile([P, P], F32)
         make_identity(nc, ident[:])
-        ident_bf = const.tile([P, P], BF16)
-        make_identity(nc, ident_bf[:])
         w_sb = const.tile([P, C_IN], BF16)
         nc.scalar.dma_start(out=w_sb[:], in_=w_rows)
         w_words = w_sb[:].bitcast(F32).rearrange("o (g p u) -> o g u p", g=PASSES, u=2)
@@ -208,12 +176,6 @@ def tile_pointwise_t_kernel(tc, x, weight, alpha_x, alpha_w, out):
                 i, g = units[u]
                 if g == 0 and i + LOAD_AHEAD < len(CHUNKS):
                     load(i + LOAD_AHEAD)
-            for ahead in range(BANKS_AHEAD, 0, -1):
-                if u + ahead < len(units) and units[u + ahead] in PE_BLOCKS:
-                    b = BANKS_AHEAD - ahead
-                    if 2 * b < PE_BLOCKS[units[u + ahead]]:
-                        regroup_bank(units[u + ahead][0], units[u + ahead][1], b)
-            if u < len(units):
                 regroup_and_sign(i, g)
             if 1 <= u <= len(units):
                 i, g = units[u - 1]

@@ -8,7 +8,7 @@ F32 = mybir.dt.float32
 U32 = mybir.dt.uint32
 U8 = mybir.dt.uint8
 FP8X4 = mybir.dt.float8_e4m3fn_x4
-SIGN = mybir.ActivationFunctionType.Sign
+COPY = mybir.ActivationFunctionType.Copy
 MULT = mybir.AluOpType.mult
 MIN = mybir.AluOpType.min
 MAX = mybir.AluOpType.max
@@ -24,12 +24,15 @@ W_MAX = 1024
 N_MAX = 512
 CHUNKS = [256, 512] + [W_MAX] * 11 + [256, 256]
 assert sum(CHUNKS) == COLS
-VECTOR_SIGNS = [(8, 1), (13, 1), (14, 0), (14, 1)]
-UP = 2.0**64
-TINY = 2.0**-69
-LOAD_AHEAD = 2
+TINY = 2.0**-133
+LIFT = 2.0**96
+LOAD_AHEAD = 3
 
 FLOPS = 2 * 2 * C_IN * C_OUT * COLS
+
+
+def on_vector(i, g):
+    return CHUNKS[i] == 256 or (i % 2 == 0 and g == 1)
 
 
 def tile_pointwise_t_kernel(tc, x, weight, alpha_x, alpha_w, out):
@@ -45,19 +48,17 @@ def tile_pointwise_t_kernel(tc, x, weight, alpha_x, alpha_w, out):
         const = stack.enter_context(tc.tile_pool(name="const", bufs=1))
         raw_pool = stack.enter_context(tc.tile_pool(name="raw", bufs=2 * (LOAD_AHEAD + 1)))
         group_pool = stack.enter_context(tc.tile_pool(name="group", bufs=5))
-        sign_pool = stack.enter_context(tc.tile_pool(name="sign", bufs=4))
+        sign_pool = stack.enter_context(tc.tile_pool(name="sign", bufs=3))
         code_pool = stack.enter_context(tc.tile_pool(name="code", bufs=5))
         res_pool = stack.enter_context(tc.tile_pool(name="res", bufs=3))
         psum_w = stack.enter_context(tc.psum_pool(name="psum_w", bufs=1))
-        psum = stack.enter_context(tc.psum_pool(name="psum", bufs=4))
-        tmp_pool = stack.enter_context(tc.tile_pool(name="tmp", bufs=2))
+        psum = stack.enter_context(tc.psum_pool(name="psum", bufs=6))
 
         raw = {}
         x_grouped = {}
         s_grouped = {}
         x_codes = {}
         s_codes = {}
-        lifted = {}
 
         def load(i):
             for g in range(PASSES):
@@ -70,36 +71,23 @@ def tile_pointwise_t_kernel(tc, x, weight, alpha_x, alpha_w, out):
                     ),
                 )
 
-        def regroup_and_sign(i, g):
+        def regroup(i, g):
             w = CHUNKS[i]
             xg = group_pool.tile([P, PACK * W_MAX], BF16, name="xg_t", tag="xg", align_bytes=64)
             x_grouped[(i, g)] = xg
+            dst = xg[:, : PACK * w].rearrange("p (c i j) -> p c j i", i=4, j=PACK)
+            src = raw[(i, g)][:, :, :w].rearrange("p j (c i) -> p c j i", i=4)
+            if on_vector(i, g):
+                nc.vector.tensor_copy(out=dst, in_=src)
+            else:
+                nc.scalar.copy(out=dst, in_=src)
+
+        def sign(i, g):
+            w = CHUNKS[i]
             sg = sign_pool.tile([P, PACK * W_MAX], BF16, name="sg_t", tag="sg", align_bytes=64)
             s_grouped[(i, g)] = sg
-            nc.vector.tensor_copy(
-                out=xg[:, : PACK * w].rearrange("p (c i j) -> p c j i", i=4, j=PACK),
-                in_=raw[(i, g)][:, :, :w].rearrange("p j (c i) -> p c j i", i=4),
-            )
-            if (i, g) not in VECTOR_SIGNS:
-                nc.scalar.activation(out=sg[:, : PACK * w], in_=xg[:, : PACK * w], func=SIGN)
-
-        def sign_on_vector_first(i, g):
-            w = CHUNKS[i]
-            big = tmp_pool.tile([P, PACK * W_MAX], BF16, name="big_t", tag="big")
-            lifted[(i, g)] = big
             nc.vector.tensor_scalar(
-                out=big[:, : PACK * w], in0=x_grouped[(i, g)][:, : PACK * w], scalar1=UP, scalar2=TINY, op0=MULT, op1=MIN
-            )
-
-        def sign_on_vector_second(i, g):
-            w = CHUNKS[i]
-            nc.vector.tensor_scalar(
-                out=s_grouped[(i, g)][:, : PACK * w],
-                in0=lifted[(i, g)][:, : PACK * w],
-                scalar1=-TINY,
-                scalar2=1.0 / TINY,
-                op0=MAX,
-                op1=MULT,
+                out=sg[:, : PACK * w], in0=x_grouped[(i, g)][:, : PACK * w], scalar1=-TINY, scalar2=TINY, op0=MAX, op1=MIN
             )
 
         def quantise(i, g, grouped, store, tag):
@@ -120,8 +108,8 @@ def tile_pointwise_t_kernel(tc, x, weight, alpha_x, alpha_w, out):
                 acc = psum.tile([P, N_MAX], F32, name="acc_t", tag="acc")
                 steps = []
                 for g in range(PASSES):
-                    steps.append((w_q, g, s_codes[(i, g)]))
                     steps.append((sw_q, g, x_codes[(i, g)]))
+                    steps.append((w_q, g, s_codes[(i, g)]))
                 for k, (stat, g, (codes, scales)) in enumerate(steps):
                     o_cols = slice(g * C_OUT, (g + 1) * C_OUT)
                     nc.tensor.matmul_mx(
@@ -133,7 +121,7 @@ def tile_pointwise_t_kernel(tc, x, weight, alpha_x, alpha_w, out):
                         start=(k == 0),
                         stop=(k == len(steps) - 1),
                     )
-                nc.scalar.copy(out=res[:, cols], in_=acc[:, :n])
+                nc.scalar.activation(out=res[:, cols], in_=acc[:, :n], func=COPY, scale=1.0 / (TINY * LIFT))
             nc.sync.dma_start(out=out_rows[:, starts[i] : starts[i] + w], in_=res[:, :w])
 
         for i in range(LOAD_AHEAD):
@@ -143,7 +131,9 @@ def tile_pointwise_t_kernel(tc, x, weight, alpha_x, alpha_w, out):
         make_identity(nc, ident[:])
         w_sb = const.tile([P, C_IN], BF16)
         nc.scalar.dma_start(out=w_sb[:], in_=w_rows)
-        w_words = w_sb[:].bitcast(F32).rearrange("o (g p u) -> o g u p", g=PASSES, u=2)
+        w_lifted = const.tile([P, C_IN], BF16)
+        nc.vector.tensor_scalar(out=w_lifted[:], in0=w_sb[:], scalar1=LIFT, scalar2=None, op0=MULT)
+        w_words = w_lifted[:].bitcast(F32).rearrange("o (g p u) -> o g u p", g=PASSES, u=2)
         w_t = psum_w.tile([P, PASSES * 2, C_OUT], F32)
         for g in range(PASSES):
             for u in range(2):
@@ -154,7 +144,9 @@ def tile_pointwise_t_kernel(tc, x, weight, alpha_x, alpha_w, out):
             out=w_grouped[:].bitcast(F32).rearrange("p (g o u) -> p g o u", g=PASSES, u=2),
             in_=w_t[:].rearrange("p (g u) o -> p g o u", u=2),
         )
-        nc.scalar.activation(out=sw_grouped[:], in_=w_grouped[:], func=SIGN)
+        nc.vector.tensor_scalar(
+            out=sw_grouped[:], in0=w_grouped[:], scalar1=-TINY * LIFT, scalar2=TINY * LIFT, op0=MAX, op1=MIN
+        )
         w_q = (
             const.tile([P, PASSES * C_OUT], U32, name="w_codes", align_bytes=64),
             const.tile([P, PASSES * C_OUT], U8, name="w_scales", align_bytes=64),
@@ -166,27 +158,21 @@ def tile_pointwise_t_kernel(tc, x, weight, alpha_x, alpha_w, out):
         nc.vector.quantize_mx(out=w_q[0][:].bitcast(FP8X4), scales=w_q[1][:], in_=w_grouped[:])
         nc.vector.quantize_mx(out=sw_q[0][:].bitcast(FP8X4), scales=sw_q[1][:], in_=sw_grouped[:])
 
-        def quantise_sign_and_multiply(i, g):
-            quantise(i, g, s_grouped, s_codes, "s")
-            if g == PASSES - 1:
-                multiply_and_store(i)
-
         for u in range(len(units) + 3):
             if u < len(units):
                 i, g = units[u]
                 if g == 0 and i + LOAD_AHEAD < len(CHUNKS):
                     load(i + LOAD_AHEAD)
-                regroup_and_sign(i, g)
-            if 1 <= u <= len(units):
-                i, g = units[u - 1]
-                quantise(i, g, x_grouped, x_codes, "x")
-                if (i, g) in VECTOR_SIGNS:
-                    sign_on_vector_first(i, g)
+                if not on_vector(i, g):
+                    regroup(i, g)
+            if 1 <= u <= len(units) and on_vector(*units[u - 1]):
+                regroup(*units[u - 1])
             if 2 <= u <= len(units) + 1:
                 i, g = units[u - 2]
-                if (i, g) in VECTOR_SIGNS:
-                    sign_on_vector_second(i, g)
-                else:
-                    quantise_sign_and_multiply(i, g)
-            if u >= 3 and units[u - 3] in VECTOR_SIGNS:
-                quantise_sign_and_multiply(units[u - 3][0], units[u - 3][1])
+                sign(i, g)
+                quantise(i, g, x_grouped, x_codes, "x")
+            if u >= 3:
+                i, g = units[u - 3]
+                quantise(i, g, s_grouped, s_codes, "s")
+                if g == PASSES - 1:
+                    multiply_and_store(i)

@@ -32,7 +32,7 @@ FLOPS = 2 * 2 * C_IN * C_OUT * COLS
 
 
 def on_vector(i, g):
-    return CHUNKS[i] == 256 or (i % 2 == 0 and g == 1)
+    return CHUNKS[i] == 256 or (i % 4 == 0 and g == 1)
 
 
 def tile_pointwise_t_kernel(tc, x, weight, alpha_x, alpha_w, out):

@@ -75,8 +75,9 @@ def tile_pointwise_t_kernel(tc, x, weight, alpha_x, alpha_w, out):
             w = CHUNKS[i]
             xg = group_pool.tile([P, PACK * W_MAX], BF16, name="xg_t", tag="xg", align_bytes=64)
             x_grouped[(i, g)] = xg
-            dst = xg[:, : PACK * w].rearrange("p (c i j) -> p c j i", i=4, j=PACK)
-            src = raw[(i, g)][:, :, :w].rearrange("p j (c i) -> p c j i", i=4)
+            run = 4 if on_vector(i, g) else 8
+            dst = xg[:, : PACK * w].rearrange("p (c i j) -> p c j i", i=run, j=PACK)
+            src = raw[(i, g)][:, :, :w].rearrange("p j (c i) -> p c j i", i=run)
             if on_vector(i, g):
                 nc.vector.tensor_copy(out=dst, in_=src)
             else:

@@ -31,8 +31,16 @@ LOAD_AHEAD = 3
 FLOPS = 2 * 2 * C_IN * C_OUT * COLS
 
 
+VECTOR_UNITS = [(4, 1), (8, 1)]
+W_PE = 256
+
+
 def on_vector(i, g):
-    return CHUNKS[i] == 256 or (i % 4 == 0 and g == 1)
+    return CHUNKS[i] == 256 or (i, g) in VECTOR_UNITS
+
+
+def pe_cols(i, g):
+    return W_PE if CHUNKS[i] == W_MAX and not on_vector(i, g) and (i, g) != (2, 0) else 0
 
 
 def tile_pointwise_t_kernel(tc, x, weight, alpha_x, alpha_w, out):
@@ -52,9 +60,11 @@ def tile_pointwise_t_kernel(tc, x, weight, alpha_x, alpha_w, out):
         code_pool = stack.enter_context(tc.tile_pool(name="code", bufs=5))
         res_pool = stack.enter_context(tc.tile_pool(name="res", bufs=3))
         psum_w = stack.enter_context(tc.psum_pool(name="psum_w", bufs=1))
-        psum = stack.enter_context(tc.psum_pool(name="psum", bufs=6))
+        psum_x = stack.enter_context(tc.psum_pool(name="psum_x", bufs=3))
+        psum = stack.enter_context(tc.psum_pool(name="psum", bufs=4))
 
         raw = {}
+        x_psum = {}
         x_grouped = {}
         s_grouped = {}
         x_codes = {}
@@ -71,17 +81,32 @@ def tile_pointwise_t_kernel(tc, x, weight, alpha_x, alpha_w, out):
                     ),
                 )
 
+        def regroup_on_tensor(i, g):
+            n = pe_cols(i, g)
+            if n:
+                bank = psum_x.tile([P, PACK * W_PE], BF16, name="bank_t", tag="bank")
+                x_psum[(i, g)] = bank
+                grouped = raw[(i, g)][:, :, :n].rearrange("p j n -> p n j")
+                for k in range(0, n, N_MAX // PACK):
+                    part = slice(k, k + N_MAX // PACK)
+                    nc.tensor.matmul(
+                        bank[:, PACK * part.start : PACK * part.stop], ident_b[:], grouped[:, part, :], start=True, stop=True
+                    )
+
         def regroup(i, g):
             w = CHUNKS[i]
             xg = group_pool.tile([P, PACK * W_MAX], BF16, name="xg_t", tag="xg", align_bytes=64)
             x_grouped[(i, g)] = xg
+            n = pe_cols(i, g)
             run = 4 if on_vector(i, g) else 8
-            dst = xg[:, : PACK * w].rearrange("p (c i j) -> p c j i", i=run, j=PACK)
-            src = raw[(i, g)][:, :, :w].rearrange("p j (c i) -> p c j i", i=run)
+            dst = xg[:, PACK * n : PACK * w].rearrange("p (c i j) -> p c j i", i=run, j=PACK)
+            src = raw[(i, g)][:, :, n:w].rearrange("p j (c i) -> p c j i", i=run)
             if on_vector(i, g):
                 nc.vector.tensor_copy(out=dst, in_=src)
             else:
                 nc.scalar.copy(out=dst, in_=src)
+            if n:
+                nc.scalar.copy(out=xg[:, : PACK * n], in_=x_psum[(i, g)][:])
 
         def sign(i, g):
             w = CHUNKS[i]
@@ -130,6 +155,8 @@ def tile_pointwise_t_kernel(tc, x, weight, alpha_x, alpha_w, out):
 
         ident = const.tile([P, P], F32)
         make_identity(nc, ident[:])
+        ident_b = const.tile([P, P], BF16)
+        make_identity(nc, ident_b[:])
         w_sb = const.tile([P, C_IN], BF16)
         nc.scalar.dma_start(out=w_sb[:], in_=w_rows)
         w_lifted = const.tile([P, C_IN], BF16)
@@ -164,6 +191,8 @@ def tile_pointwise_t_kernel(tc, x, weight, alpha_x, alpha_w, out):
                 i, g = units[u]
                 if g == 0 and i + LOAD_AHEAD < len(CHUNKS):
                     load(i + LOAD_AHEAD)
+                if u + 1 < len(units):
+                    regroup_on_tensor(*units[u + 1])
                 if not on_vector(i, g):
                     regroup(i, g)
             if 1 <= u <= len(units) and on_vector(*units[u - 1]):

@@ -31,16 +31,16 @@ LOAD_AHEAD = 3
 FLOPS = 2 * 2 * C_IN * C_OUT * COLS
 
 
-VECTOR_UNITS = [(4, 1), (8, 1)]
+VECTOR_UNITS = [(2, 0), (4, 0), (7, 0), (10, 0)]
 W_PE = 256
 
 
 def on_vector(i, g):
-    return CHUNKS[i] == 256 or (i, g) in VECTOR_UNITS
+    return (i, g) in VECTOR_UNITS
 
 
 def pe_cols(i, g):
-    return W_PE if CHUNKS[i] == W_MAX and not on_vector(i, g) and (i, g) != (2, 0) else 0
+    return W_PE if CHUNKS[i] == W_MAX and not on_vector(i, g) else 0
 
 
 def tile_pointwise_t_kernel(tc, x, weight, alpha_x, alpha_w, out):
@@ -69,6 +69,7 @@ def tile_pointwise_t_kernel(tc, x, weight, alpha_x, alpha_w, out):
         s_grouped = {}
         x_codes = {}
         s_codes = {}
+        banks = {}
 
         def load(i):
             for g in range(PASSES):
@@ -125,13 +126,14 @@ def tile_pointwise_t_kernel(tc, x, weight, alpha_x, alpha_w, out):
                 out=codes[:, :w].bitcast(FP8X4), scales=scales[:, :w], in_=grouped[(i, g)][:, : PACK * w]
             )
 
-        def multiply_and_store(i):
+        def multiply(i):
             w = CHUNKS[i]
             n = min(w, N_MAX)
-            res = res_pool.tile([P, W_MAX], F32, name="res_t", tag="res")
+            banks[i] = []
             for h in range(w // n):
                 cols = slice(h * n, (h + 1) * n)
                 acc = psum.tile([P, N_MAX], F32, name="acc_t", tag="acc")
+                banks[i].append(acc)
                 steps = []
                 for g in range(PASSES):
                     steps.append((sw_q, g, x_codes[(i, g)]))
@@ -147,7 +149,15 @@ def tile_pointwise_t_kernel(tc, x, weight, alpha_x, alpha_w, out):
                         start=(k == 0),
                         stop=(k == len(steps) - 1),
                     )
-                nc.scalar.activation(out=res[:, cols], in_=acc[:, :n], func=COPY, scale=1.0 / (TINY * LIFT))
+
+        def empty_and_store(i):
+            w = CHUNKS[i]
+            n = min(w, N_MAX)
+            res = res_pool.tile([P, W_MAX], F32, name="res_t", tag="res")
+            for h, acc in enumerate(banks[i]):
+                nc.scalar.activation(
+                    out=res[:, h * n : (h + 1) * n], in_=acc[:, :n], func=COPY, scale=1.0 / (TINY * LIFT)
+                )
             nc.sync.dma_start(out=out_rows[:, starts[i] : starts[i] + w], in_=res[:, :w])
 
         for i in range(LOAD_AHEAD):
@@ -186,7 +196,7 @@ def tile_pointwise_t_kernel(tc, x, weight, alpha_x, alpha_w, out):
         nc.vector.quantize_mx(out=w_q[0][:].bitcast(FP8X4), scales=w_q[1][:], in_=w_grouped[:])
         nc.vector.quantize_mx(out=sw_q[0][:].bitcast(FP8X4), scales=sw_q[1][:], in_=sw_grouped[:])
 
-        for u in range(len(units) + 3):
+        for u in range(len(units) + 4):
             if u < len(units):
                 i, g = units[u]
                 if g == 0 and i + LOAD_AHEAD < len(CHUNKS):
@@ -201,8 +211,10 @@ def tile_pointwise_t_kernel(tc, x, weight, alpha_x, alpha_w, out):
                 i, g = units[u - 2]
                 sign(i, g)
                 quantise(i, g, x_grouped, x_codes, "x")
-            if u >= 3:
+            if 3 <= u <= len(units) + 2:
                 i, g = units[u - 3]
                 quantise(i, g, s_grouped, s_codes, "s")
                 if g == PASSES - 1:
-                    multiply_and_store(i)
+                    multiply(i)
+            if u >= 4 and units[u - 4][1] == PASSES - 1:
+                empty_and_store(units[u - 4][0])

@@ -55,8 +55,8 @@ def tile_pointwise_t_kernel(tc, x, weight, alpha_x, alpha_w, out):
     with ExitStack() as stack:
         const = stack.enter_context(tc.tile_pool(name="const", bufs=1))
         raw_pool = stack.enter_context(tc.tile_pool(name="raw", bufs=2 * (LOAD_AHEAD + 1)))
-        group_pool = stack.enter_context(tc.tile_pool(name="group", bufs=5))
-        sign_pool = stack.enter_context(tc.tile_pool(name="sign", bufs=3))
+        group_pool = stack.enter_context(tc.tile_pool(name="group", bufs=7))
+        sign_pool = stack.enter_context(tc.tile_pool(name="sign", bufs=4))
         code_pool = stack.enter_context(tc.tile_pool(name="code", bufs=5))
         res_pool = stack.enter_context(tc.tile_pool(name="res", bufs=3))
         psum_w = stack.enter_context(tc.psum_pool(name="psum_w", bufs=1))
@@ -67,8 +67,7 @@ def tile_pointwise_t_kernel(tc, x, weight, alpha_x, alpha_w, out):
         x_psum = {}
         x_grouped = {}
         s_grouped = {}
-        x_codes = {}
-        s_codes = {}
+        quantised = {}
         banks = {}
 
         def load(i):
@@ -117,13 +116,20 @@ def tile_pointwise_t_kernel(tc, x, weight, alpha_x, alpha_w, out):
                 out=sg[:, : PACK * w], in0=x_grouped[(i, g)][:, : PACK * w], scalar1=-TINY, scalar2=TINY, op0=MAX, op1=MIN
             )
 
-        def quantise(i, g, grouped, store, tag):
+        def quantise_x(i, g):
             w = CHUNKS[i]
-            codes = code_pool.tile([P, W_MAX], U32, name=tag + "_codes", tag=tag + "c", align_bytes=64)
-            scales = code_pool.tile([P, W_MAX], U8, name=tag + "_scales", tag=tag + "s", align_bytes=64)
-            store[(i, g)] = (codes, scales)
+            codes = code_pool.tile([P, 2, W_MAX], U32, name="codes_t", tag="codes", align_bytes=64)
+            scales = code_pool.tile([P, 2, W_MAX], U8, name="scales_t", tag="scales", align_bytes=64)
+            quantised[(i, g)] = (codes, scales)
             nc.vector.quantize_mx(
-                out=codes[:, :w].bitcast(FP8X4), scales=scales[:, :w], in_=grouped[(i, g)][:, : PACK * w]
+                out=codes[:, 0, :w].bitcast(FP8X4), scales=scales[:, 0, :w], in_=x_grouped[(i, g)][:, : PACK * w]
+            )
+
+        def quantise_sign(i, g):
+            w = CHUNKS[i]
+            codes, scales = quantised[(i, g)]
+            nc.vector.quantize_mx(
+                out=codes[:, 1, :w].bitcast(FP8X4), scales=scales[:, 1, :w], in_=s_grouped[(i, g)][:, : PACK * w]
             )
 
         def multiply(i):
@@ -136,16 +142,17 @@ def tile_pointwise_t_kernel(tc, x, weight, alpha_x, alpha_w, out):
                 banks[i].append(acc)
                 steps = []
                 for g in range(PASSES):
-                    steps.append((sw_q, g, x_codes[(i, g)]))
-                    steps.append((w_q, g, s_codes[(i, g)]))
-                for k, (stat, g, (codes, scales)) in enumerate(steps):
+                    steps.append((sw_q, g, 0))
+                    steps.append((w_q, g, 1))
+                for k, (stat, g, half) in enumerate(steps):
+                    codes, scales = quantised[(i, g)]
                     o_cols = slice(g * C_OUT, (g + 1) * C_OUT)
                     nc.tensor.matmul_mx(
                         out=acc[:, :n],
                         lhsT=stat[0][:, o_cols].bitcast(FP8X4),
                         lhsT_scale=stat[1][:, o_cols],
-                        rhs=codes[:, cols].bitcast(FP8X4),
-                        rhs_scale=scales[:, cols],
+                        rhs=codes[:, half, cols].bitcast(FP8X4),
+                        rhs_scale=scales[:, half, cols],
                         start=(k == 0),
                         stop=(k == len(steps) - 1),
                     )
@@ -169,19 +176,21 @@ def tile_pointwise_t_kernel(tc, x, weight, alpha_x, alpha_w, out):
         make_identity(nc, ident_b[:])
         w_sb = const.tile([P, C_IN], BF16)
         nc.scalar.dma_start(out=w_sb[:], in_=w_rows)
-        w_lifted = const.tile([P, C_IN], BF16)
-        nc.vector.tensor_scalar(out=w_lifted[:], in0=w_sb[:], scalar1=LIFT, scalar2=None, op0=MULT)
-        w_words = w_lifted[:].bitcast(F32).rearrange("o (g p u) -> o g u p", g=PASSES, u=2)
+        w_words = w_sb[:].bitcast(F32).rearrange("o (g p u) -> o g u p", g=PASSES, u=2)
         w_t = psum_w.tile([P, PASSES * 2, C_OUT], F32)
         for g in range(PASSES):
             for u in range(2):
                 nc.tensor.transpose(w_t[:, 2 * g + u, :], w_words[:, g, u, :], ident[:])
         w_grouped = const.tile([P, PASSES * C_OUT * PACK], BF16, align_bytes=64)
         sw_grouped = const.tile([P, PASSES * C_OUT * PACK], BF16, align_bytes=64)
-        nc.vector.tensor_copy(
-            out=w_grouped[:].bitcast(F32).rearrange("p (g o u) -> p g o u", g=PASSES, u=2),
-            in_=w_t[:].rearrange("p (g u) o -> p g o u", u=2),
-        )
+        for g in range(PASSES):
+            nc.vector.tensor_scalar(
+                out=w_grouped[:, g * C_OUT * PACK : (g + 1) * C_OUT * PACK].rearrange("p (o u e) -> p o u e", u=2, e=2),
+                in0=w_t[:, 2 * g : 2 * g + 2, :].bitcast(BF16).rearrange("p u (o e) -> p o u e", e=2),
+                scalar1=LIFT,
+                scalar2=None,
+                op0=MULT,
+            )
         nc.vector.tensor_scalar(
             out=sw_grouped[:], in0=w_grouped[:], scalar1=-TINY * LIFT, scalar2=TINY * LIFT, op0=MAX, op1=MIN
         )
@@ -210,10 +219,10 @@ def tile_pointwise_t_kernel(tc, x, weight, alpha_x, alpha_w, out):
             if 2 <= u <= len(units) + 1:
                 i, g = units[u - 2]
                 sign(i, g)
-                quantise(i, g, x_grouped, x_codes, "x")
+                quantise_x(i, g)
             if 3 <= u <= len(units) + 2:
                 i, g = units[u - 3]
-                quantise(i, g, s_grouped, s_codes, "s")
+                quantise_sign(i, g)
                 if g == PASSES - 1:
                     multiply(i)
             if u >= 4 and units[u - 4][1] == PASSES - 1:

@@ -31,7 +31,7 @@ LOAD_AHEAD = 3
 FLOPS = 2 * 2 * C_IN * C_OUT * COLS
 
 
-VECTOR_UNITS = [(2, 0), (4, 0), (7, 0), (10, 0)]
+VECTOR_UNITS = [(0, 0), (2, 0), (5, 0), (9, 0)]
 W_PE = 256
 
 
@@ -167,6 +167,8 @@ def tile_pointwise_t_kernel(tc, x, weight, alpha_x, alpha_w, out):
                 )
             nc.sync.dma_start(out=out_rows[:, starts[i] : starts[i] + w], in_=res[:, :w])
 
+        w_sb = const.tile([P, C_IN], BF16)
+        nc.sync.dma_start(out=w_sb[:], in_=w_rows)
         for i in range(LOAD_AHEAD):
             load(i)
 
@@ -174,8 +176,6 @@ def tile_pointwise_t_kernel(tc, x, weight, alpha_x, alpha_w, out):
         make_identity(nc, ident[:])
         ident_b = const.tile([P, P], BF16)
         make_identity(nc, ident_b[:])
-        w_sb = const.tile([P, C_IN], BF16)
-        nc.scalar.dma_start(out=w_sb[:], in_=w_rows)
         w_words = w_sb[:].bitcast(F32).rearrange("o (g p u) -> o g u p", g=PASSES, u=2)
         w_t = psum_w.tile([P, PASSES * 2, C_OUT], F32)
         for g in range(PASSES):

@@ -9,7 +9,6 @@ U32 = mybir.dt.uint32
 U8 = mybir.dt.uint8
 FP8X4 = mybir.dt.float8_e4m3fn_x4
 COPY = mybir.ActivationFunctionType.Copy
-MULT = mybir.AluOpType.mult
 MIN = mybir.AluOpType.min
 MAX = mybir.AluOpType.max
 
@@ -167,9 +166,10 @@ def tile_pointwise_t_kernel(tc, x, weight, alpha_x, alpha_w, out):
                 )
             nc.sync.dma_start(out=out_rows[:, starts[i] : starts[i] + w], in_=res[:, :w])
 
+        load(0)
         w_sb = const.tile([P, C_IN], BF16)
         nc.sync.dma_start(out=w_sb[:], in_=w_rows)
-        for i in range(LOAD_AHEAD):
+        for i in range(1, LOAD_AHEAD):
             load(i)
 
         ident = const.tile([P, P], F32)
@@ -184,12 +184,11 @@ def tile_pointwise_t_kernel(tc, x, weight, alpha_x, alpha_w, out):
         w_grouped = const.tile([P, PASSES * C_OUT * PACK], BF16, align_bytes=64)
         sw_grouped = const.tile([P, PASSES * C_OUT * PACK], BF16, align_bytes=64)
         for g in range(PASSES):
-            nc.vector.tensor_scalar(
+            nc.scalar.activation(
                 out=w_grouped[:, g * C_OUT * PACK : (g + 1) * C_OUT * PACK].rearrange("p (o u e) -> p o u e", u=2, e=2),
-                in0=w_t[:, 2 * g : 2 * g + 2, :].bitcast(BF16).rearrange("p u (o e) -> p o u e", e=2),
-                scalar1=LIFT,
-                scalar2=None,
-                op0=MULT,
+                in_=w_t[:, 2 * g : 2 * g + 2, :].bitcast(BF16).rearrange("p u (o e) -> p o u e", e=2),
+                func=COPY,
+                scale=LIFT,
             )
         nc.vector.tensor_scalar(
             out=sw_grouped[:], in0=w_grouped[:], scalar1=-TINY * LIFT, scalar2=TINY * LIFT, op0=MAX, op1=MIN

from contextlib import ExitStack

import concourse.mybir as mybir
from concourse.masks import make_identity

BF16 = mybir.dt.bfloat16
F32 = mybir.dt.float32
U32 = mybir.dt.uint32
U8 = mybir.dt.uint8
FP8X4 = mybir.dt.float8_e4m3fn_x4
COPY = mybir.ActivationFunctionType.Copy
MIN = mybir.AluOpType.min
MAX = mybir.AluOpType.max

P = 128
PACK = 4
K_PASS = P * PACK
C_IN = 1024
C_OUT = 128
PASSES = C_IN // K_PASS
COLS = 112 * 112
W_MAX = 1024
N_MAX = 512
CHUNKS = [256, 512] + [W_MAX] * 11 + [256, 256]
assert sum(CHUNKS) == COLS
TINY = 2.0**-133
LIFT = 2.0**96
LOAD_AHEAD = 3

FLOPS = 2 * 2 * C_IN * C_OUT * COLS


VECTOR_UNITS = [(0, 0), (2, 0), (5, 0), (9, 0)]
W_PE = 256


def on_vector(i, g):
    return (i, g) in VECTOR_UNITS


def pe_cols(i, g):
    return W_PE if CHUNKS[i] == W_MAX and not on_vector(i, g) else 0


def tile_pointwise_t_kernel(tc, x, weight, alpha_x, alpha_w, out):
    nc = tc.nc
    x_rows = x.rearrange("b c h w -> (b c) (h w)")
    w_rows = weight.rearrange("o c a b -> o (c a b)")
    out_rows = out.rearrange("b o h w -> (b o) (h w)")

    starts = [sum(CHUNKS[:i]) for i in range(len(CHUNKS))]
    units = [(i, g) for i in range(len(CHUNKS)) for g in range(PASSES)]

    with ExitStack() as stack:
        const = stack.enter_context(tc.tile_pool(name="const", bufs=1))
        raw_pool = stack.enter_context(tc.tile_pool(name="raw", bufs=2 * (LOAD_AHEAD + 1)))
        group_pool = stack.enter_context(tc.tile_pool(name="group", bufs=7))
        sign_pool = stack.enter_context(tc.tile_pool(name="sign", bufs=4))
        code_pool = stack.enter_context(tc.tile_pool(name="code", bufs=5))
        res_pool = stack.enter_context(tc.tile_pool(name="res", bufs=3))
        psum_w = stack.enter_context(tc.psum_pool(name="psum_w", bufs=1))
        psum_x = stack.enter_context(tc.psum_pool(name="psum_x", bufs=3))
        psum = stack.enter_context(tc.psum_pool(name="psum", bufs=4))

        raw = {}
        x_psum = {}
        x_grouped = {}
        s_grouped = {}
        quantised = {}
        banks = {}

        def load(i):
            for g in range(PASSES):
                t = raw_pool.tile([P, PACK, W_MAX], BF16, name="raw_t", tag="raw")
                raw[(i, g)] = t
                nc.sync.dma_start(
                    out=t[:, :, : CHUNKS[i]],
                    in_=x_rows[K_PASS * g : K_PASS * (g + 1), starts[i] : starts[i] + CHUNKS[i]].rearrange(
                        "(p j) w -> p j w", j=PACK
                    ),
                )

        def regroup_on_tensor(i, g):
            n = pe_cols(i, g)
            if n:
                bank = psum_x.tile([P, PACK * W_PE], BF16, name="bank_t", tag="bank")
                x_psum[(i, g)] = bank
                grouped = raw[(i, g)][:, :, :n].rearrange("p j n -> p n j")
                for k in range(0, n, N_MAX // PACK):
                    part = slice(k, k + N_MAX // PACK)
                    nc.tensor.matmul(
                        bank[:, PACK * part.start : PACK * part.stop], ident_b[:], grouped[:, part, :], start=True, stop=True
                    )

        def regroup(i, g):
            w = CHUNKS[i]
            xg = group_pool.tile([P, PACK * W_MAX], BF16, name="xg_t", tag="xg", align_bytes=64)
            x_grouped[(i, g)] = xg
            n = pe_cols(i, g)
            run = 4 if on_vector(i, g) else 8
            dst = xg[:, PACK * n : PACK * w].rearrange("p (c i j) -> p c j i", i=run, j=PACK)
            src = raw[(i, g)][:, :, n:w].rearrange("p j (c i) -> p c j i", i=run)
            if on_vector(i, g):
                nc.vector.tensor_copy(out=dst, in_=src)
            else:
                nc.scalar.copy(out=dst, in_=src)
            if n:
                nc.scalar.copy(out=xg[:, : PACK * n], in_=x_psum[(i, g)][:])

        def sign(i, g):
            w = CHUNKS[i]
            sg = sign_pool.tile([P, PACK * W_MAX], BF16, name="sg_t", tag="sg", align_bytes=64)
            s_grouped[(i, g)] = sg
            nc.vector.tensor_scalar(
                out=sg[:, : PACK * w], in0=x_grouped[(i, g)][:, : PACK * w], scalar1=-TINY, scalar2=TINY, op0=MAX, op1=MIN
            )

        def quantise_x(i, g):
            w = CHUNKS[i]
            codes = code_pool.tile([P, 2, W_MAX], U32, name="codes_t", tag="codes", align_bytes=64)
            scales = code_pool.tile([P, 2, W_MAX], U8, name="scales_t", tag="scales", align_bytes=64)
            quantised[(i, g)] = (codes, scales)
            nc.vector.quantize_mx(
                out=codes[:, 0, :w].bitcast(FP8X4), scales=scales[:, 0, :w], in_=x_grouped[(i, g)][:, : PACK * w]
            )

        def quantise_sign(i, g):
            w = CHUNKS[i]
            codes, scales = quantised[(i, g)]
            nc.vector.quantize_mx(
                out=codes[:, 1, :w].bitcast(FP8X4), scales=scales[:, 1, :w], in_=s_grouped[(i, g)][:, : PACK * w]
            )

        def multiply(i):
            w = CHUNKS[i]
            n = min(w, N_MAX)
            banks[i] = []
            for h in range(w // n):
                cols = slice(h * n, (h + 1) * n)
                acc = psum.tile([P, N_MAX], F32, name="acc_t", tag="acc")
                banks[i].append(acc)
                steps = []
                for g in range(PASSES):
                    steps.append((sw_q, g, 0))
                    steps.append((w_q, g, 1))
                for k, (stat, g, half) in enumerate(steps):
                    codes, scales = quantised[(i, g)]
                    o_cols = slice(g * C_OUT, (g + 1) * C_OUT)
                    nc.tensor.matmul_mx(
                        out=acc[:, :n],
                        lhsT=stat[0][:, o_cols].bitcast(FP8X4),
                        lhsT_scale=stat[1][:, o_cols],
                        rhs=codes[:, half, cols].bitcast(FP8X4),
                        rhs_scale=scales[:, half, cols],
                        start=(k == 0),
                        stop=(k == len(steps) - 1),
                    )

        def empty_and_store(i):
            w = CHUNKS[i]
            n = min(w, N_MAX)
            res = res_pool.tile([P, W_MAX], F32, name="res_t", tag="res")
            for h, acc in enumerate(banks[i]):
                nc.scalar.activation(
                    out=res[:, h * n : (h + 1) * n], in_=acc[:, :n], func=COPY, scale=1.0 / (TINY * LIFT)
                )
            nc.sync.dma_start(out=out_rows[:, starts[i] : starts[i] + w], in_=res[:, :w])

        load(0)
        w_sb = const.tile([P, C_IN], BF16)
        nc.sync.dma_start(out=w_sb[:], in_=w_rows)
        for i in range(1, LOAD_AHEAD):
            load(i)

        ident = const.tile([P, P], F32)
        make_identity(nc, ident[:])
        ident_b = const.tile([P, P], BF16)
        make_identity(nc, ident_b[:])
        w_words = w_sb[:].bitcast(F32).rearrange("o (g p u) -> o g u p", g=PASSES, u=2)
        w_t = psum_w.tile([P, PASSES * 2, C_OUT], F32)
        for g in range(PASSES):
            for u in range(2):
                nc.tensor.transpose(w_t[:, 2 * g + u, :], w_words[:, g, u, :], ident[:])
        w_grouped = const.tile([P, PASSES * C_OUT * PACK], BF16, align_bytes=64)
        sw_grouped = const.tile([P, PASSES * C_OUT * PACK], BF16, align_bytes=64)
        for g in range(PASSES):
            nc.scalar.activation(
                out=w_grouped[:, g * C_OUT * PACK : (g + 1) * C_OUT * PACK].rearrange("p (o u e) -> p o u e", u=2, e=2),
                in_=w_t[:, 2 * g : 2 * g + 2, :].bitcast(BF16).rearrange("p u (o e) -> p o u e", e=2),
                func=COPY,
                scale=LIFT,
            )
        nc.vector.tensor_scalar(
            out=sw_grouped[:], in0=w_grouped[:], scalar1=-TINY * LIFT, scalar2=TINY * LIFT, op0=MAX, op1=MIN
        )
        w_q = (
            const.tile([P, PASSES * C_OUT], U32, name="w_codes", align_bytes=64),
            const.tile([P, PASSES * C_OUT], U8, name="w_scales", align_bytes=64),
        )
        sw_q = (
            const.tile([P, PASSES * C_OUT], U32, name="sw_codes", align_bytes=64),
            const.tile([P, PASSES * C_OUT], U8, name="sw_scales", align_bytes=64),
        )
        nc.vector.quantize_mx(out=w_q[0][:].bitcast(FP8X4), scales=w_q[1][:], in_=w_grouped[:])
        nc.vector.quantize_mx(out=sw_q[0][:].bitcast(FP8X4), scales=sw_q[1][:], in_=sw_grouped[:])

        for u in range(len(units) + 4):
            if u < len(units):
                i, g = units[u]
                if g == 0 and i + LOAD_AHEAD < len(CHUNKS):
                    load(i + LOAD_AHEAD)
                if u + 1 < len(units):
                    regroup_on_tensor(*units[u + 1])
                if not on_vector(i, g):
                    regroup(i, g)
            if 1 <= u <= len(units) and on_vector(*units[u - 1]):
                regroup(*units[u - 1])
            if 2 <= u <= len(units) + 1:
                i, g = units[u - 2]
                sign(i, g)
                quantise_x(i, g)
            if 3 <= u <= len(units) + 2:
                i, g = units[u - 3]
                quantise_sign(i, g)
                if g == PASSES - 1:
                    multiply(i)
            if u >= 4 and units[u - 4][1] == PASSES - 1:
                empty_and_store(units[u - 4][0])
